import numpy as np
import ml_dtypes


def mxq(x, axis, fmt="e4m3"):
    dtype, down = {"e4m3": (ml_dtypes.float8_e4m3fn, 7), "e5m2": (ml_dtypes.float8_e5m2, 14)}[fmt]
    v = np.moveaxis(np.asarray(x, np.float32).astype(ml_dtypes.bfloat16).astype(np.float64), axis, -1)
    blocks = v.reshape(v.shape[:-1] + (-1, 32))
    amax = np.abs(blocks).max(-1, keepdims=True)
    byte = np.maximum(np.where(amax > 0, np.frexp(amax)[1] - 1 + 127, 0) - down, 1)
    scale = np.exp2(byte - 127.0)
    codes = (blocks / scale).astype(np.float32).astype(dtype).astype(np.float64)
    return np.moveaxis((codes * scale).reshape(v.shape), -1, axis)


WIDE = False


def mx_kscale(k):
    if not WIDE:
        return np.ones(k)
    levels = np.array([10, -10, 5, -5, 0])
    a = np.random.permutation(np.resize(levels, k // 512 * 4)).reshape(k // 512, 4)
    idx = np.arange(k)
    return np.exp2(a[idx // 512, idx % 128 // 32])


BF16 = ml_dtypes.bfloat16


def bf(x):
    return np.asarray(x, np.float32).astype(BF16)


def f64(x):
    return np.asarray(x).astype(np.float64)


B, N, D, F1, F2, F3, G1, G2 = 4, 32, 512, 512, 1024, 512, 512, 512
ALPHA = 0.2


def lrelu(v):
    return np.maximum(v, ALPHA * v)


def setup_inputs():
    s, t = mx_kscale(D), mx_kscale(F1)
    ss = np.concatenate([s, s])
    return {"x": bf(np.random.standard_normal((B, N, D)) * s),
            "fe_w0": bf(np.random.standard_normal((D + D, F1)) / np.sqrt(D + D) / ss[:, None] * t),
            "fe_b0": bf(np.random.standard_normal(F1) * 0.3 * t),
            "fe_w1": bf(np.random.standard_normal((F1, F2)) * 1.4 / np.sqrt(F1) / t[:, None]),
            "fe_b1": bf(np.random.standard_normal(F2) * 0.3)}


def reference(x, fe_w0, fe_b0, fe_w1, fe_b1):
    xq = mxq(f64(x), 2, "e4m3")
    w0 = f64(fe_w0)
    u = xq @ mxq(w0[:D], 0, "e4m3")
    v = xq @ mxq(w0[D:], 0, "e4m3")
    e1 = lrelu(u[:, :, None, :] + v[:, None, :, :] + f64(fe_b0))
    return lrelu((mxq(e1, 3, "e4m3") @ mxq(f64(fe_w1), 0, "e4m3")) + f64(fe_b1))

@@ -1,0 +1,230 @@
+from contextlib import ExitStack
+
+import concourse.mybir as mybir
+from concourse.masks import make_identity
+
+F32 = mybir.dt.float32
+BF16 = mybir.dt.bfloat16
+U32 = mybir.dt.uint32
+U8 = mybir.dt.uint8
+FP8X4 = mybir.dt.float8_e4m3fn_x4
+ALU = mybir.AluOpType
+ACT = mybir.ActivationFunctionType
+
+ALPHA = 0.2
+
+P = 128
+PACK = 4
+K = P * PACK
+GRAPHS = 4
+N = 32
+NODES = GRAPHS * N
+PAIRS = GRAPHS * N * N
+F1 = 512
+F2 = 1024
+BANK = 512
+
+CHUNK_I = 8
+CHUNK = CHUNK_I * N
+CHUNKS = PAIRS // CHUNK
+ROUND_PAIRS = BANK
+ROUND_BLOCKS = BANK // P
+HALVES = F2 // BANK
+ROUNDS = (PAIRS // ROUND_PAIRS) * HALVES
+CHUNKS_AHEAD = 3
+
+FLOPS = 2 * (2 * NODES * K * F1) + 2 * PAIRS * K * F2
+
+
+def tile_graph_gan_pa_kernel(tc, x, fe_w0, fe_b0, fe_w1, fe_b1, out):
+    nc = tc.nc
+    out_rows = out.flatten_outer_dims()
+
+    with ExitStack() as stack:
+        stack.enter_context(tc.manual_schedule())
+        keep = stack.enter_context(tc.tile_pool(name="keep", bufs=1))
+        work = stack.enter_context(tc.tile_pool(name="work", bufs=2))
+        biased = stack.enter_context(tc.tile_pool(name="biased", bufs=2 * ROUND_BLOCKS))
+        result = stack.enter_context(tc.tile_pool(name="result", bufs=6))
+        sums = stack.enter_context(tc.psum_pool(name="sums", bufs=4))
+        turned = stack.enter_context(tc.psum_pool(name="turned", bufs=4))
+
+        x_rows = keep.tile([NODES, K], BF16)
+        nc.sync.dma_start(out=x_rows[:], in_=x.flatten_outer_dims())
+
+        def load_weight(block, name):
+            raw = keep.tile([P, PACK, BANK], BF16, name=name)
+            nc.sync.dma_start(out=raw[:], in_=block.rearrange("(t p) f -> p t f", p=P))
+            return raw
+
+        w0_raw = [load_weight(fe_w0[h * K : (h + 1) * K, :], "w0_raw%d" % h) for h in range(2)]
+        w1_raw = [load_weight(fe_w1[:, h * BANK : (h + 1) * BANK], "w1_raw%d" % h) for h in range(HALVES)]
+
+        bias_rows = keep.tile([P, P], BF16)
+        nc.vector.memset(bias_rows[:], 0.0)
+        B0_ROWS = F1 // P
+        B1_ROWS = F2 // P
+        nc.scalar.dma_start(out=bias_rows[0:B0_ROWS, :], in_=fe_b0.rearrange("(r c) -> r c", c=P))
+        nc.scalar.dma_start(
+            out=bias_rows[B0_ROWS : B0_ROWS + B1_ROWS, :], in_=fe_b1.rearrange("(r c) -> r c", c=P)
+        )
+
+        ident_bf = keep.tile([P, P], BF16)
+        make_identity(nc, ident_bf[:])
+        ident_f32 = keep.tile([P, P], F32)
+        make_identity(nc, ident_f32[:])
+
+        def quantise(grouped, width, name):
+            codes = keep.tile([P, width], U32, name=name + "_codes", align_bytes=64)
+            scales = keep.tile([P, width], U8, name=name + "_scales", align_bytes=64)
+            nc.vector.quantize_mx(out=codes[:].bitcast(FP8X4), scales=scales[:], in_=grouped)
+            return codes, scales
+
+        def regroup_weight(copy, raw, name):
+            grouped = keep.tile([P, BANK, PACK], BF16, name=name, align_bytes=64)
+            copy(out=grouped[:], in_=raw[:].rearrange("p t f -> p f t"))
+            return grouped[:].rearrange("p f t -> p (f t)")
+
+        x_turned = turned.tile([P, PACK, NODES], BF16, tag="turned")
+        for t in range(PACK):
+            nc.tensor.transpose(x_turned[:, t, :], x_rows[:, t * P : (t + 1) * P], ident_bf[:])
+        x_grouped = keep.tile([P, NODES, PACK], BF16, align_bytes=64)
+        nc.vector.tensor_copy(out=x_grouped[:], in_=x_turned[:].rearrange("p t n -> p n t"))
+
+        w0_grouped0 = regroup_weight(nc.vector.tensor_copy, w0_raw[0], "w0_grouped0")
+        x_codes, x_scales = quantise(x_grouped[:].rearrange("p n t -> p (n t)"), NODES, "x")
+        w0_grouped1 = regroup_weight(nc.vector.tensor_copy, w0_raw[1], "w0_grouped1")
+        w0_q = [quantise(w0_grouped0, F1, "w0a"), quantise(w0_grouped1, F1, "w0b")]
+
+        products = []
+        for h in range(2):
+            codes, scales = w0_q[h]
+            product = sums.tile([P, PACK, NODES], F32, tag="sums")
+            for t in range(PACK):
+                nc.tensor.matmul_mx(
+                    out=product[:, t, :],
+                    lhsT=codes[:, t * P : (t + 1) * P].bitcast(FP8X4),
+                    lhsT_scale=scales[:, t * P : (t + 1) * P],
+                    rhs=x_codes[:].bitcast(FP8X4),
+                    rhs_scale=x_scales[:],
+                    start=True,
+                    stop=True,
+                )
+            products.append(product)
+
+        bias_turned = turned.tile([P, P], BF16, tag="turned")
+        nc.tensor.transpose(bias_turned[:], bias_rows[:], ident_bf[:])
+        bias = keep.tile([P, B0_ROWS + B1_ROWS], F32)
+        nc.vector.tensor_copy(out=bias[:], in_=bias_turned[:, 0 : B0_ROWS + B1_ROWS])
+
+        u_b0 = keep.tile([P, NODES, PACK], F32)
+        nc.vector.tensor_tensor(
+            out=u_b0[:],
+            in0=products[0][:].rearrange("p t n -> p n t"),
+            in1=bias[:, 0:B0_ROWS].unsqueeze(1).to_broadcast([P, NODES, PACK]),
+            op=ALU.add,
+        )
+        v_sb = keep.tile([P, NODES, PACK], F32)
+        nc.scalar.copy(out=v_sb[:], in_=products[1][:].rearrange("p t n -> p n t"))
+
+        w1_grouped = [regroup_weight(nc.scalar.copy, w1_raw[h], "w1_grouped%d" % h) for h in range(HALVES)]
+
+        e1_codes = keep.tile([P, PAIRS], U32, align_bytes=64)
+        e1_scales = keep.tile([P, PAIRS], U8, align_bytes=64)
+
+        def e1_values(m):
+            b, i0 = divmod(m * CHUNK_I, N)
+            shape = [P, CHUNK_I, N, PACK]
+            pre = work.tile(shape, F32, tag="pre")
+            nc.vector.tensor_tensor(
+                out=pre[:],
+                in0=u_b0[:, b * N + i0 : b * N + i0 + CHUNK_I, :].unsqueeze(2).to_broadcast(shape),
+                in1=v_sb[:, b * N : (b + 1) * N, :].unsqueeze(1).to_broadcast(shape),
+                op=ALU.add,
+            )
+            pre_flat = pre[:].rearrange("p i j t -> p (i j t)")
+            e1 = work.tile([P, CHUNK * PACK], BF16, tag="e1", align_bytes=64)
+            nc.vector.scalar_tensor_tensor(
+                out=e1[:], in0=pre_flat, scalar=ALPHA, in1=pre_flat, op0=ALU.mult, op1=ALU.max
+            )
+            return e1
+
+        def e1_quantise(m, e1):
+            cols = slice(m * CHUNK, (m + 1) * CHUNK)
+            nc.vector.quantize_mx(out=e1_codes[:, cols].bitcast(FP8X4), scales=e1_scales[:, cols], in_=e1[:])
+
+        def multiply(n):
+            pairs, half = divmod(n, HALVES)
+            codes, scales = w1_q[half]
+            cols = slice(pairs * ROUND_PAIRS, (pairs + 1) * ROUND_PAIRS)
+            banks = []
+            for k in range(ROUND_BLOCKS):
+                acc = sums.tile([P, ROUND_PAIRS], F32, tag="sums")
+                nc.tensor.matmul_mx(
+                    out=acc[:],
+                    lhsT=codes[:, k * P : (k + 1) * P].bitcast(FP8X4),
+                    lhsT_scale=scales[:, k * P : (k + 1) * P],
+                    rhs=e1_codes[:, cols].bitcast(FP8X4),
+                    rhs_scale=e1_scales[:, cols],
+                    start=True,
+                    stop=True,
+                )
+                banks.append(acc)
+            return banks
+
+        def add_bias(n, banks):
+            half = n % HALVES
+            tiles = []
+            for k in range(ROUND_BLOCKS):
+                column = B0_ROWS + half * ROUND_BLOCKS + k
+                z = biased.tile([P, ROUND_PAIRS], F32, tag="z")
+                nc.scalar.activation(
+                    out=z[:], in_=banks[k][:], func=ACT.Identity, bias=bias[:, column : column + 1], scale=1.0
+                )
+                tiles.append(z)
+            return tiles
+
+        def turn(tiles):
+            banks = []
+            for s in range(ROUND_BLOCKS):
+                z_turned = turned.tile([P, BANK], F32, tag="turned")
+                for k in range(ROUND_BLOCKS):
+                    nc.tensor.transpose(
+                        z_turned[:, k * P : (k + 1) * P], tiles[k][:, s * P : (s + 1) * P], ident_f32[:]
+                    )
+                banks.append(z_turned)
+            return banks
+
+        def lrelu_and_store(n, s, z_turned):
+            pairs, half = divmod(n, HALVES)
+            scaled = result.tile([P, BANK], F32, tag="scaled")
+            nc.scalar.mul(out=scaled[:], in_=z_turned[:], mul=ALPHA)
+            res = result.tile([P, BANK], F32, tag="res")
+            nc.vector.tensor_tensor(out=res[:], in0=z_turned[:], in1=scaled[:], op=ALU.max)
+            row0 = pairs * ROUND_PAIRS + s * P
+            nc.sync.dma_start(out=out_rows[row0 : row0 + P, half * BANK : (half + 1) * BANK], in_=res[:])
+
+        first = e1_values(0)
+        w1_q = [quantise(w1_grouped[0], BANK, "w1a")]
+        second = e1_values(1)
+        e1_quantise(0, first)
+        e1_quantise(1, second)
+        banks = multiply(0)
+        z_tiles = add_bias(0, banks)
+        third = e1_values(2)
+        w1_q.append(quantise(w1_grouped[1], BANK, "w1b"))
+        e1_quantise(2, third)
+
+        for n in range(ROUNDS):
+            m = n + CHUNKS_AHEAD
+            if m < CHUNKS:
+                e1 = e1_values(m)
+            if n + 1 < ROUNDS:
+                banks = multiply(n + 1)
+            turned_banks = turn(z_tiles)
+            if n + 1 < ROUNDS:
+                z_tiles = add_bias(n + 1, banks)
+            for s in range(ROUND_BLOCKS):
+                if s == ROUND_BLOCKS // 2 and m < CHUNKS:
+                    e1_quantise(m, e1)
+                lrelu_and_store(n, s, turned_banks[s])

@@ -31,7 +31,7 @@ ROUND_PAIRS = BANK
 ROUND_BLOCKS = BANK // P
 HALVES = F2 // BANK
 ROUNDS = (PAIRS // ROUND_PAIRS) * HALVES
-CHUNKS_AHEAD = 3
+CHUNKS_AHEAD = 4
 
 FLOPS = 2 * (2 * NODES * K * F1) + 2 * PAIRS * K * F2
 
@@ -135,8 +135,8 @@ def tile_graph_gan_pa_kernel(tc, x, fe_w0, fe_b0, fe_w1, fe_b1, out):
         def e1_values(m):
             b, i0 = divmod(m * CHUNK_I, N)
             shape = [P, CHUNK_I, N, PACK]
-            pre = work.tile(shape, F32, tag="pre")
-            nc.vector.tensor_tensor(
+            pre = work.tile(shape, F32, tag="pre", bufs=3)
+            nc.gpsimd.tensor_tensor(
                 out=pre[:],
                 in0=u_b0[:, b * N + i0 : b * N + i0 + CHUNK_I, :].unsqueeze(2).to_broadcast(shape),
                 in1=v_sb[:, b * N : (b + 1) * N, :].unsqueeze(1).to_broadcast(shape),
@@ -204,16 +204,18 @@ def tile_graph_gan_pa_kernel(tc, x, fe_w0, fe_b0, fe_w1, fe_b1, out):
             row0 = pairs * ROUND_PAIRS + s * P
             nc.sync.dma_start(out=out_rows[row0 : row0 + P, half * BANK : (half + 1) * BANK], in_=res[:])
 
-        first = e1_values(0)
+        early = [e1_values(0)]
         w1_q = [quantise(w1_grouped[0], BANK, "w1a")]
-        second = e1_values(1)
-        e1_quantise(0, first)
-        e1_quantise(1, second)
+        early.append(e1_values(1))
+        e1_quantise(0, early[0])
+        e1_quantise(1, early[1])
         banks = multiply(0)
         z_tiles = add_bias(0, banks)
-        third = e1_values(2)
+        early.append(e1_values(2))
         w1_q.append(quantise(w1_grouped[1], BANK, "w1b"))
-        e1_quantise(2, third)
+        early.append(e1_values(3))
+        e1_quantise(2, early[2])
+        e1_quantise(3, early[3])
 
         for n in range(ROUNDS):
             m = n + CHUNKS_AHEAD
@@ -225,6 +227,6 @@ def tile_graph_gan_pa_kernel(tc, x, fe_w0, fe_b0, fe_w1, fe_b1, out):
             if n + 1 < ROUNDS:
                 z_tiles = add_bias(n + 1, banks)
             for s in range(ROUND_BLOCKS):
-                if s == ROUND_BLOCKS // 2 and m < CHUNKS:
-                    e1_quantise(m, e1)
                 lrelu_and_store(n, s, turned_banks[s])
+            if m < CHUNKS:
+                e1_quantise(m, e1)

@@ -31,6 +31,7 @@ ROUND_PAIRS = BANK
 ROUND_BLOCKS = BANK // P
 HALVES = F2 // BANK
 ROUNDS = (PAIRS // ROUND_PAIRS) * HALVES
+SCALAR_BLOCKS = 3
 CHUNKS_AHEAD = 4
 
 FLOPS = 2 * (2 * NODES * K * F1) + 2 * PAIRS * K * F2
@@ -178,9 +179,12 @@ def tile_graph_gan_pa_kernel(tc, x, fe_w0, fe_b0, fe_w1, fe_b1, out):
             for k in range(ROUND_BLOCKS):
                 column = B0_ROWS + half * ROUND_BLOCKS + k
                 z = biased.tile([P, ROUND_PAIRS], F32, tag="z")
-                nc.scalar.activation(
-                    out=z[:], in_=banks[k][:], func=ACT.Identity, bias=bias[:, column : column + 1], scale=1.0
-                )
+                if k < SCALAR_BLOCKS:
+                    nc.scalar.activation(
+                        out=z[:], in_=banks[k][:], func=ACT.Identity, bias=bias[:, column : column + 1], scale=1.0
+                    )
+                else:
+                    nc.vector.tensor_scalar_add(out=z[:], in0=banks[k][:], scalar1=bias[:, column : column + 1])
                 tiles.append(z)
             return tiles
 
@@ -210,9 +214,9 @@ def tile_graph_gan_pa_kernel(tc, x, fe_w0, fe_b0, fe_w1, fe_b1, out):
         e1_quantise(0, early[0])
         e1_quantise(1, early[1])
         banks = multiply(0)
-        z_tiles = add_bias(0, banks)
         early.append(e1_values(2))
         w1_q.append(quantise(w1_grouped[1], BANK, "w1b"))
+        z_tiles = add_bias(0, banks)
         early.append(e1_values(3))
         e1_quantise(2, early[2])
         e1_quantise(3, early[3])

@@ -31,7 +31,6 @@ ROUND_PAIRS = BANK
 ROUND_BLOCKS = BANK // P
 HALVES = F2 // BANK
 ROUNDS = (PAIRS // ROUND_PAIRS) * HALVES
-SCALAR_BLOCKS = 3
 CHUNKS_AHEAD = 4
 
 FLOPS = 2 * (2 * NODES * K * F1) + 2 * PAIRS * K * F2
@@ -134,10 +133,11 @@ def tile_graph_gan_pa_kernel(tc, x, fe_w0, fe_b0, fe_w1, fe_b1, out):
         e1_scales = keep.tile([P, PAIRS], U8, align_bytes=64)
 
         def e1_values(m):
+            adder = nc.vector if m <= CHUNKS_AHEAD else nc.gpsimd
             b, i0 = divmod(m * CHUNK_I, N)
             shape = [P, CHUNK_I, N, PACK]
             pre = work.tile(shape, F32, tag="pre", bufs=3)
-            nc.gpsimd.tensor_tensor(
+            adder.tensor_tensor(
                 out=pre[:],
                 in0=u_b0[:, b * N + i0 : b * N + i0 + CHUNK_I, :].unsqueeze(2).to_broadcast(shape),
                 in1=v_sb[:, b * N : (b + 1) * N, :].unsqueeze(1).to_broadcast(shape),
@@ -175,11 +175,12 @@ def tile_graph_gan_pa_kernel(tc, x, fe_w0, fe_b0, fe_w1, fe_b1, out):
 
         def add_bias(n, banks):
             half = n % HALVES
+            scalar_blocks = ROUND_BLOCKS - n % 2
             tiles = []
             for k in range(ROUND_BLOCKS):
                 column = B0_ROWS + half * ROUND_BLOCKS + k
                 z = biased.tile([P, ROUND_PAIRS], F32, tag="z")
-                if k < SCALAR_BLOCKS:
+                if k < scalar_blocks:
                     nc.scalar.activation(
                         out=z[:], in_=banks[k][:], func=ACT.Identity, bias=bias[:, column : column + 1], scale=1.0
                     )
@@ -214,9 +215,9 @@ def tile_graph_gan_pa_kernel(tc, x, fe_w0, fe_b0, fe_w1, fe_b1, out):
         e1_quantise(0, early[0])
         e1_quantise(1, early[1])
         banks = multiply(0)
-        early.append(e1_values(2))
-        w1_q.append(quantise(w1_grouped[1], BANK, "w1b"))
         z_tiles = add_bias(0, banks)
+        w1_q.append(quantise(w1_grouped[1], BANK, "w1b"))
+        early.append(e1_values(2))
         early.append(e1_values(3))
         e1_quantise(2, early[2])
         e1_quantise(3, early[3])

@@ -31,6 +31,7 @@ ROUND_PAIRS = BANK
 ROUND_BLOCKS = BANK // P
 HALVES = F2 // BANK
 ROUNDS = (PAIRS // ROUND_PAIRS) * HALVES
+SCALAR_BANKS = 3
 CHUNKS_AHEAD = 4
 
 FLOPS = 2 * (2 * NODES * K * F1) + 2 * PAIRS * K * F2
@@ -44,7 +45,7 @@ def tile_graph_gan_pa_kernel(tc, x, fe_w0, fe_b0, fe_w1, fe_b1, out):
         stack.enter_context(tc.manual_schedule())
         keep = stack.enter_context(tc.tile_pool(name="keep", bufs=1))
         work = stack.enter_context(tc.tile_pool(name="work", bufs=2))
-        biased = stack.enter_context(tc.tile_pool(name="biased", bufs=2 * ROUND_BLOCKS))
+        biased = stack.enter_context(tc.tile_pool(name="biased", bufs=2))
         result = stack.enter_context(tc.tile_pool(name="result", bufs=6))
         sums = stack.enter_context(tc.psum_pool(name="sums", bufs=4))
         turned = stack.enter_context(tc.psum_pool(name="turned", bufs=4))
@@ -133,11 +134,10 @@ def tile_graph_gan_pa_kernel(tc, x, fe_w0, fe_b0, fe_w1, fe_b1, out):
         e1_scales = keep.tile([P, PAIRS], U8, align_bytes=64)
 
         def e1_values(m):
-            adder = nc.vector if m <= CHUNKS_AHEAD else nc.gpsimd
             b, i0 = divmod(m * CHUNK_I, N)
             shape = [P, CHUNK_I, N, PACK]
-            pre = work.tile(shape, F32, tag="pre", bufs=3)
-            adder.tensor_tensor(
+            pre = work.tile(shape, F32, tag="pre")
+            nc.vector.tensor_tensor(
                 out=pre[:],
                 in0=u_b0[:, b * N + i0 : b * N + i0 + CHUNK_I, :].unsqueeze(2).to_broadcast(shape),
                 in1=v_sb[:, b * N : (b + 1) * N, :].unsqueeze(1).to_broadcast(shape),
@@ -155,9 +155,9 @@ def tile_graph_gan_pa_kernel(tc, x, fe_w0, fe_b0, fe_w1, fe_b1, out):
             nc.vector.quantize_mx(out=e1_codes[:, cols].bitcast(FP8X4), scales=e1_scales[:, cols], in_=e1[:])
 
         def multiply(n):
-            pairs, half = divmod(n, HALVES)
+            group, half = divmod(n, HALVES)
             codes, scales = w1_q[half]
-            cols = slice(pairs * ROUND_PAIRS, (pairs + 1) * ROUND_PAIRS)
+            cols = slice(group * ROUND_PAIRS, (group + 1) * ROUND_PAIRS)
             banks = []
             for k in range(ROUND_BLOCKS):
                 acc = sums.tile([P, ROUND_PAIRS], F32, tag="sums")
@@ -175,38 +175,46 @@ def tile_graph_gan_pa_kernel(tc, x, fe_w0, fe_b0, fe_w1, fe_b1, out):
 
         def add_bias(n, banks):
             half = n % HALVES
-            scalar_blocks = ROUND_BLOCKS - n % 2
-            tiles = []
+            z = biased.tile([P, ROUND_BLOCKS, ROUND_PAIRS], F32, tag="z")
             for k in range(ROUND_BLOCKS):
                 column = B0_ROWS + half * ROUND_BLOCKS + k
-                z = biased.tile([P, ROUND_PAIRS], F32, tag="z")
-                if k < scalar_blocks:
-                    nc.scalar.activation(
-                        out=z[:], in_=banks[k][:], func=ACT.Identity, bias=bias[:, column : column + 1], scale=1.0
-                    )
-                else:
-                    nc.vector.tensor_scalar_add(out=z[:], in0=banks[k][:], scalar1=bias[:, column : column + 1])
-                tiles.append(z)
-            return tiles
+                nc.scalar.activation(
+                    out=z[:, k, :], in_=banks[k][:], func=ACT.Identity, bias=bias[:, column : column + 1], scale=1.0
+                )
+            return z
 
-        def turn(tiles):
-            banks = []
+        def lrelu_rest(z):
+            rest = biased.tile([P, ROUND_BLOCKS, ROUND_PAIRS], F32, tag="rest")
+            nc.vector.tensor_scalar(
+                out=rest[:], in0=z[:], scalar1=ALPHA - 1.0, scalar2=0.0, op0=ALU.mult, op1=ALU.max
+            )
+            return rest
+
+        def turn_and_add(z, rest):
+            turned_banks = []
             for s in range(ROUND_BLOCKS):
-                z_turned = turned.tile([P, BANK], F32, tag="turned")
+                lrelu_z = turned.tile([P, BANK], F32, tag="turned")
                 for k in range(ROUND_BLOCKS):
-                    nc.tensor.transpose(
-                        z_turned[:, k * P : (k + 1) * P], tiles[k][:, s * P : (s + 1) * P], ident_f32[:]
-                    )
-                banks.append(z_turned)
-            return banks
+                    for term in (z, rest):
+                        nc.tensor.matmul(
+                            out=lrelu_z[:, k * P : (k + 1) * P],
+                            lhsT=term[:, k, s * P : (s + 1) * P],
+                            rhs=ident_f32[:],
+                            is_transpose=True,
+                            start=(term is z),
+                            stop=(term is rest),
+                        )
+                turned_banks.append(lrelu_z)
+            return turned_banks
 
-        def lrelu_and_store(n, s, z_turned):
-            pairs, half = divmod(n, HALVES)
-            scaled = result.tile([P, BANK], F32, tag="scaled")
-            nc.scalar.mul(out=scaled[:], in_=z_turned[:], mul=ALPHA)
+        def copy_and_store(n, s, lrelu_z):
+            group, half = divmod(n, HALVES)
             res = result.tile([P, BANK], F32, tag="res")
-            nc.vector.tensor_tensor(out=res[:], in0=z_turned[:], in1=scaled[:], op=ALU.max)
-            row0 = pairs * ROUND_PAIRS + s * P
+            if s < SCALAR_BANKS:
+                nc.scalar.copy(out=res[:], in_=lrelu_z[:])
+            else:
+                nc.vector.tensor_copy(out=res[:], in_=lrelu_z[:])
+            row0 = group * ROUND_PAIRS + s * P
             nc.sync.dma_start(out=out_rows[row0 : row0 + P, half * BANK : (half + 1) * BANK], in_=res[:])
 
         early = [e1_values(0)]
@@ -215,9 +223,10 @@ def tile_graph_gan_pa_kernel(tc, x, fe_w0, fe_b0, fe_w1, fe_b1, out):
         e1_quantise(0, early[0])
         e1_quantise(1, early[1])
         banks = multiply(0)
-        z_tiles = add_bias(0, banks)
+        z = add_bias(0, banks)
         w1_q.append(quantise(w1_grouped[1], BANK, "w1b"))
         early.append(e1_values(2))
+        rest = lrelu_rest(z)
         early.append(e1_values(3))
         e1_quantise(2, early[2])
         e1_quantise(3, early[3])
@@ -228,10 +237,11 @@ def tile_graph_gan_pa_kernel(tc, x, fe_w0, fe_b0, fe_w1, fe_b1, out):
                 e1 = e1_values(m)
             if n + 1 < ROUNDS:
                 banks = multiply(n + 1)
-            turned_banks = turn(z_tiles)
+            turned_banks = turn_and_add(z, rest)
             if n + 1 < ROUNDS:
-                z_tiles = add_bias(n + 1, banks)
+                z = add_bias(n + 1, banks)
+                rest = lrelu_rest(z)
             for s in range(ROUND_BLOCKS):
-                lrelu_and_store(n, s, turned_banks[s])
+                copy_and_store(n, s, turned_banks[s])
             if m < CHUNKS:
                 e1_quantise(m, e1)

@@ -31,7 +31,6 @@ ROUND_PAIRS = BANK
 ROUND_BLOCKS = BANK // P
 HALVES = F2 // BANK
 ROUNDS = (PAIRS // ROUND_PAIRS) * HALVES
-SCALAR_BANKS = 3
 CHUNKS_AHEAD = 4
 
 FLOPS = 2 * (2 * NODES * K * F1) + 2 * PAIRS * K * F2
@@ -42,10 +41,9 @@ def tile_graph_gan_pa_kernel(tc, x, fe_w0, fe_b0, fe_w1, fe_b1, out):
     out_rows = out.flatten_outer_dims()
 
     with ExitStack() as stack:
-        stack.enter_context(tc.manual_schedule())
         keep = stack.enter_context(tc.tile_pool(name="keep", bufs=1))
         work = stack.enter_context(tc.tile_pool(name="work", bufs=2))
-        biased = stack.enter_context(tc.tile_pool(name="biased", bufs=2))
+        biased = stack.enter_context(tc.tile_pool(name="biased", bufs=2 * ROUND_BLOCKS))
         result = stack.enter_context(tc.tile_pool(name="result", bufs=6))
         sums = stack.enter_context(tc.psum_pool(name="sums", bufs=4))
         turned = stack.enter_context(tc.psum_pool(name="turned", bufs=4))
@@ -134,10 +132,11 @@ def tile_graph_gan_pa_kernel(tc, x, fe_w0, fe_b0, fe_w1, fe_b1, out):
         e1_scales = keep.tile([P, PAIRS], U8, align_bytes=64)
 
         def e1_values(m):
+            adder = nc.vector if m <= CHUNKS_AHEAD else nc.gpsimd
             b, i0 = divmod(m * CHUNK_I, N)
             shape = [P, CHUNK_I, N, PACK]
-            pre = work.tile(shape, F32, tag="pre")
-            nc.vector.tensor_tensor(
+            pre = work.tile(shape, F32, tag="pre", bufs=3)
+            adder.tensor_tensor(
                 out=pre[:],
                 in0=u_b0[:, b * N + i0 : b * N + i0 + CHUNK_I, :].unsqueeze(2).to_broadcast(shape),
                 in1=v_sb[:, b * N : (b + 1) * N, :].unsqueeze(1).to_broadcast(shape),
@@ -155,9 +154,9 @@ def tile_graph_gan_pa_kernel(tc, x, fe_w0, fe_b0, fe_w1, fe_b1, out):
             nc.vector.quantize_mx(out=e1_codes[:, cols].bitcast(FP8X4), scales=e1_scales[:, cols], in_=e1[:])
 
         def multiply(n):
-            group, half = divmod(n, HALVES)
+            pairs, half = divmod(n, HALVES)
             codes, scales = w1_q[half]
-            cols = slice(group * ROUND_PAIRS, (group + 1) * ROUND_PAIRS)
+            cols = slice(pairs * ROUND_PAIRS, (pairs + 1) * ROUND_PAIRS)
             banks = []
             for k in range(ROUND_BLOCKS):
                 acc = sums.tile([P, ROUND_PAIRS], F32, tag="sums")
@@ -175,46 +174,38 @@ def tile_graph_gan_pa_kernel(tc, x, fe_w0, fe_b0, fe_w1, fe_b1, out):
 
         def add_bias(n, banks):
             half = n % HALVES
-            z = biased.tile([P, ROUND_BLOCKS, ROUND_PAIRS], F32, tag="z")
+            scalar_blocks = ROUND_BLOCKS - n % 2
+            tiles = []
             for k in range(ROUND_BLOCKS):
                 column = B0_ROWS + half * ROUND_BLOCKS + k
-                nc.scalar.activation(
-                    out=z[:, k, :], in_=banks[k][:], func=ACT.Identity, bias=bias[:, column : column + 1], scale=1.0
-                )
-            return z
+                z = biased.tile([P, ROUND_PAIRS], F32, tag="z")
+                if k < scalar_blocks:
+                    nc.scalar.activation(
+                        out=z[:], in_=banks[k][:], func=ACT.Identity, bias=bias[:, column : column + 1], scale=1.0
+                    )
+                else:
+                    nc.vector.tensor_scalar_add(out=z[:], in0=banks[k][:], scalar1=bias[:, column : column + 1])
+                tiles.append(z)
+            return tiles
 
-        def lrelu_rest(z):
-            rest = biased.tile([P, ROUND_BLOCKS, ROUND_PAIRS], F32, tag="rest")
-            nc.vector.tensor_scalar(
-                out=rest[:], in0=z[:], scalar1=ALPHA - 1.0, scalar2=0.0, op0=ALU.mult, op1=ALU.max
-            )
-            return rest
-
-        def turn_and_add(z, rest):
-            turned_banks = []
+        def turn(tiles):
+            banks = []
             for s in range(ROUND_BLOCKS):
-                lrelu_z = turned.tile([P, BANK], F32, tag="turned")
+                z_turned = turned.tile([P, BANK], F32, tag="turned")
                 for k in range(ROUND_BLOCKS):
-                    for term in (z, rest):
-                        nc.tensor.matmul(
-                            out=lrelu_z[:, k * P : (k + 1) * P],
-                            lhsT=term[:, k, s * P : (s + 1) * P],
-                            rhs=ident_f32[:],
-                            is_transpose=True,
-                            start=(term is z),
-                            stop=(term is rest),
-                        )
-                turned_banks.append(lrelu_z)
-            return turned_banks
+                    nc.tensor.transpose(
+                        z_turned[:, k * P : (k + 1) * P], tiles[k][:, s * P : (s + 1) * P], ident_f32[:]
+                    )
+                banks.append(z_turned)
+            return banks
 
-        def copy_and_store(n, s, lrelu_z):
-            group, half = divmod(n, HALVES)
+        def lrelu_and_store(n, s, z_turned):
+            pairs, half = divmod(n, HALVES)
+            scaled = result.tile([P, BANK], F32, tag="scaled")
+            nc.scalar.mul(out=scaled[:], in_=z_turned[:], mul=ALPHA)
             res = result.tile([P, BANK], F32, tag="res")
-            if s < SCALAR_BANKS:
-                nc.scalar.copy(out=res[:], in_=lrelu_z[:])
-            else:
-                nc.vector.tensor_copy(out=res[:], in_=lrelu_z[:])
-            row0 = group * ROUND_PAIRS + s * P
+            nc.vector.tensor_tensor(out=res[:], in0=z_turned[:], in1=scaled[:], op=ALU.max)
+            row0 = pairs * ROUND_PAIRS + s * P
             nc.sync.dma_start(out=out_rows[row0 : row0 + P, half * BANK : (half + 1) * BANK], in_=res[:])
 
         early = [e1_values(0)]
@@ -223,10 +214,9 @@ def tile_graph_gan_pa_kernel(tc, x, fe_w0, fe_b0, fe_w1, fe_b1, out):
         e1_quantise(0, early[0])
         e1_quantise(1, early[1])
         banks = multiply(0)
-        z = add_bias(0, banks)
+        z_tiles = add_bias(0, banks)
         w1_q.append(quantise(w1_grouped[1], BANK, "w1b"))
         early.append(e1_values(2))
-        rest = lrelu_rest(z)
         early.append(e1_values(3))
         e1_quantise(2, early[2])
         e1_quantise(3, early[3])
@@ -237,11 +227,10 @@ def tile_graph_gan_pa_kernel(tc, x, fe_w0, fe_b0, fe_w1, fe_b1, out):
                 e1 = e1_values(m)
             if n + 1 < ROUNDS:
                 banks = multiply(n + 1)
-            turned_banks = turn_and_add(z, rest)
+            turned_banks = turn(z_tiles)
             if n + 1 < ROUNDS:
-                z = add_bias(n + 1, banks)
-                rest = lrelu_rest(z)
+                z_tiles = add_bias(n + 1, banks)
             for s in range(ROUND_BLOCKS):
-                copy_and_store(n, s, turned_banks[s])
+                lrelu_and_store(n, s, turned_banks[s])
             if m < CHUNKS:
                 e1_quantise(m, e1)

@@ -124,9 +124,10 @@ def tile_graph_gan_pa_kernel(tc, x, fe_w0, fe_b0, fe_w1, fe_b1, out):
             op=ALU.add,
         )
         v_sb = keep.tile([P, NODES, PACK], F32)
-        nc.scalar.copy(out=v_sb[:], in_=products[1][:].rearrange("p t n -> p n t"))
-
-        w1_grouped = [regroup_weight(nc.scalar.copy, w1_raw[h], "w1_grouped%d" % h) for h in range(HALVES)]
+        with tc.manual_schedule(engines={mybir.EngineType.Activation}):
+            w1_grouped = [regroup_weight(nc.scalar.copy, w1_raw[0], "w1_grouped0")]
+            nc.scalar.copy(out=v_sb[:], in_=products[1][:].rearrange("p t n -> p n t"))
+            w1_grouped.append(regroup_weight(nc.scalar.copy, w1_raw[1], "w1_grouped1"))
 
         e1_codes = keep.tile([P, PAIRS], U32, align_bytes=64)
         e1_scales = keep.tile([P, PAIRS], U8, align_bytes=64)
@@ -174,7 +175,10 @@ def tile_graph_gan_pa_kernel(tc, x, fe_w0, fe_b0, fe_w1, fe_b1, out):
 
         def add_bias(n, banks):
             half = n % HALVES
-            scalar_blocks = ROUND_BLOCKS - n % 2
+            if n + CHUNKS_AHEAD > CHUNKS:
+                scalar_blocks = ROUND_BLOCKS - 2
+            else:
+                scalar_blocks = ROUND_BLOCKS - n % 2
             tiles = []
             for k in range(ROUND_BLOCKS):
                 column = B0_ROWS + half * ROUND_BLOCKS + k

@@ -81,7 +81,10 @@ def tile_graph_gan_pa_kernel(tc, x, fe_w0, fe_b0, fe_w1, fe_b1, out):
 
         def regroup_weight(copy, raw, name):
             grouped = keep.tile([P, BANK, PACK], BF16, name=name, align_bytes=64)
-            copy(out=grouped[:], in_=raw[:].rearrange("p t f -> p f t"))
+            copy(
+                out=grouped[:].rearrange("p (c i) t -> p c t i", i=PACK),
+                in_=raw[:].rearrange("p t (c i) -> p c t i", i=PACK),
+            )
             return grouped[:].rearrange("p f t -> p (f t)")
 
         x_turned = turned.tile([P, PACK, NODES], BF16, tag="turned")

@@ -139,7 +139,10 @@ def tile_graph_gan_pa_kernel(tc, x, fe_w0, fe_b0, fe_w1, fe_b1, out):
             adder = nc.vector if m <= CHUNKS_AHEAD else nc.gpsimd
             b, i0 = divmod(m * CHUNK_I, N)
             shape = [P, CHUNK_I, N, PACK]
-            pre = work.tile(shape, F32, tag="pre", bufs=3)
+            if m < CHUNKS_AHEAD:
+                pre = work.tile(shape, F32, tag="pre_start", bufs=2)
+            else:
+                pre = work.tile(shape, F32, tag="pre_round", bufs=1)
             adder.tensor_tensor(
                 out=pre[:],
                 in0=u_b0[:, b * N + i0 : b * N + i0 + CHUNK_I, :].unsqueeze(2).to_broadcast(shape),

@@ -182,19 +182,28 @@ def tile_graph_gan_pa_kernel(tc, x, fe_w0, fe_b0, fe_w1, fe_b1, out):
         def add_bias(n, banks):
             half = n % HALVES
             if n + CHUNKS_AHEAD > CHUNKS:
-                scalar_blocks = ROUND_BLOCKS - 2
+                vector_cols = 2 * ROUND_PAIRS
+            elif n > 0:
+                vector_cols = ROUND_PAIRS // 2
             else:
-                scalar_blocks = ROUND_BLOCKS - n % 2
+                vector_cols = 0
             tiles = []
             for k in range(ROUND_BLOCKS):
                 column = B0_ROWS + half * ROUND_BLOCKS + k
                 z = biased.tile([P, ROUND_PAIRS], F32, tag="z")
-                if k < scalar_blocks:
+                split = min(max((ROUND_BLOCKS - k) * ROUND_PAIRS - vector_cols, 0), ROUND_PAIRS)
+                if split > 0:
                     nc.scalar.activation(
-                        out=z[:], in_=banks[k][:], func=ACT.Identity, bias=bias[:, column : column + 1], scale=1.0
+                        out=z[:, 0:split],
+                        in_=banks[k][:, 0:split],
+                        func=ACT.Identity,
+                        bias=bias[:, column : column + 1],
+                        scale=1.0,
                     )
-                else:
-                    nc.vector.tensor_scalar_add(out=z[:], in0=banks[k][:], scalar1=bias[:, column : column + 1])
+                if split < ROUND_PAIRS:
+                    nc.vector.tensor_scalar_add(
+                        out=z[:, split:ROUND_PAIRS], in0=banks[k][:, split:ROUND_PAIRS], scalar1=bias[:, column : column + 1]
+                    )
                 tiles.append(z)
             return tiles
 

@@ -184,7 +184,7 @@ def tile_graph_gan_pa_kernel(tc, x, fe_w0, fe_b0, fe_w1, fe_b1, out):
             if n + CHUNKS_AHEAD > CHUNKS:
                 vector_cols = 2 * ROUND_PAIRS
             elif n > 0:
-                vector_cols = ROUND_PAIRS // 2
+                vector_cols = 3 * ROUND_PAIRS // 4
             else:
                 vector_cols = 0
             tiles = []

from contextlib import ExitStack

import concourse.mybir as mybir
from concourse.masks import make_identity

F32 = mybir.dt.float32
BF16 = mybir.dt.bfloat16
U32 = mybir.dt.uint32
U8 = mybir.dt.uint8
FP8X4 = mybir.dt.float8_e4m3fn_x4
ALU = mybir.AluOpType
ACT = mybir.ActivationFunctionType

ALPHA = 0.2

P = 128
PACK = 4
K = P * PACK
GRAPHS = 4
N = 32
NODES = GRAPHS * N
PAIRS = GRAPHS * N * N
F1 = 512
F2 = 1024
BANK = 512

CHUNK_I = 8
CHUNK = CHUNK_I * N
CHUNKS = PAIRS // CHUNK
ROUND_PAIRS = BANK
ROUND_BLOCKS = BANK // P
HALVES = F2 // BANK
ROUNDS = (PAIRS // ROUND_PAIRS) * HALVES
CHUNKS_AHEAD = 4

FLOPS = 2 * (2 * NODES * K * F1) + 2 * PAIRS * K * F2


def tile_graph_gan_pa_kernel(tc, x, fe_w0, fe_b0, fe_w1, fe_b1, out):
    nc = tc.nc
    out_rows = out.flatten_outer_dims()

    with ExitStack() as stack:
        keep = stack.enter_context(tc.tile_pool(name="keep", bufs=1))
        work = stack.enter_context(tc.tile_pool(name="work", bufs=2))
        biased = stack.enter_context(tc.tile_pool(name="biased", bufs=2 * ROUND_BLOCKS))
        result = stack.enter_context(tc.tile_pool(name="result", bufs=6))
        sums = stack.enter_context(tc.psum_pool(name="sums", bufs=4))
        turned = stack.enter_context(tc.psum_pool(name="turned", bufs=4))

        x_rows = keep.tile([NODES, K], BF16)
        nc.sync.dma_start(out=x_rows[:], in_=x.flatten_outer_dims())

        def load_weight(block, name):
            raw = keep.tile([P, PACK, BANK], BF16, name=name)
            nc.sync.dma_start(out=raw[:], in_=block.rearrange("(t p) f -> p t f", p=P))
            return raw

        w0_raw = [load_weight(fe_w0[h * K : (h + 1) * K, :], "w0_raw%d" % h) for h in range(2)]
        w1_raw = [load_weight(fe_w1[:, h * BANK : (h + 1) * BANK], "w1_raw%d" % h) for h in range(HALVES)]

        bias_rows = keep.tile([P, P], BF16)
        nc.vector.memset(bias_rows[:], 0.0)
        B0_ROWS = F1 // P
        B1_ROWS = F2 // P
        nc.scalar.dma_start(out=bias_rows[0:B0_ROWS, :], in_=fe_b0.rearrange("(r c) -> r c", c=P))
        nc.scalar.dma_start(
            out=bias_rows[B0_ROWS : B0_ROWS + B1_ROWS, :], in_=fe_b1.rearrange("(r c) -> r c", c=P)
        )

        ident_bf = keep.tile([P, P], BF16)
        make_identity(nc, ident_bf[:])
        ident_f32 = keep.tile([P, P], F32)
        make_identity(nc, ident_f32[:])

        def quantise(grouped, width, name):
            codes = keep.tile([P, width], U32, name=name + "_codes", align_bytes=64)
            scales = keep.tile([P, width], U8, name=name + "_scales", align_bytes=64)
            nc.vector.quantize_mx(out=codes[:].bitcast(FP8X4), scales=scales[:], in_=grouped)
            return codes, scales

        def regroup_weight(copy, raw, name):
            grouped = keep.tile([P, BANK, PACK], BF16, name=name, align_bytes=64)
            copy(
                out=grouped[:].rearrange("p (c i) t -> p c t i", i=PACK),
                in_=raw[:].rearrange("p t (c i) -> p c t i", i=PACK),
            )
            return grouped[:].rearrange("p f t -> p (f t)")

        x_turned = turned.tile([P, PACK, NODES], BF16, tag="turned")
        for t in range(PACK):
            nc.tensor.transpose(x_turned[:, t, :], x_rows[:, t * P : (t + 1) * P], ident_bf[:])
        x_grouped = keep.tile([P, NODES, PACK], BF16, align_bytes=64)
        nc.vector.tensor_copy(out=x_grouped[:], in_=x_turned[:].rearrange("p t n -> p n t"))

        w0_grouped0 = regroup_weight(nc.vector.tensor_copy, w0_raw[0], "w0_grouped0")
        x_codes, x_scales = quantise(x_grouped[:].rearrange("p n t -> p (n t)"), NODES, "x")
        w0_grouped1 = regroup_weight(nc.vector.tensor_copy, w0_raw[1], "w0_grouped1")
        w0_q = [quantise(w0_grouped0, F1, "w0a"), quantise(w0_grouped1, F1, "w0b")]

        products = []
        for h in range(2):
            codes, scales = w0_q[h]
            product = sums.tile([P, PACK, NODES], F32, tag="sums")
            for t in range(PACK):
                nc.tensor.matmul_mx(
                    out=product[:, t, :],
                    lhsT=codes[:, t * P : (t + 1) * P].bitcast(FP8X4),
                    lhsT_scale=scales[:, t * P : (t + 1) * P],
                    rhs=x_codes[:].bitcast(FP8X4),
                    rhs_scale=x_scales[:],
                    start=True,
                    stop=True,
                )
            products.append(product)

        bias_turned = turned.tile([P, P], BF16, tag="turned")
        nc.tensor.transpose(bias_turned[:], bias_rows[:], ident_bf[:])
        bias = keep.tile([P, B0_ROWS + B1_ROWS], F32)
        nc.vector.tensor_copy(out=bias[:], in_=bias_turned[:, 0 : B0_ROWS + B1_ROWS])

        u_b0 = keep.tile([P, NODES, PACK], F32)
        nc.vector.tensor_tensor(
            out=u_b0[:],
            in0=products[0][:].rearrange("p t n -> p n t"),
            in1=bias[:, 0:B0_ROWS].unsqueeze(1).to_broadcast([P, NODES, PACK]),
            op=ALU.add,
        )
        v_sb = keep.tile([P, NODES, PACK], F32)
        with tc.manual_schedule(engines={mybir.EngineType.Activation}):
            w1_grouped = [regroup_weight(nc.scalar.copy, w1_raw[0], "w1_grouped0")]
            nc.scalar.copy(out=v_sb[:], in_=products[1][:].rearrange("p t n -> p n t"))
            w1_grouped.append(regroup_weight(nc.scalar.copy, w1_raw[1], "w1_grouped1"))

        e1_codes = keep.tile([P, PAIRS], U32, align_bytes=64)
        e1_scales = keep.tile([P, PAIRS], U8, align_bytes=64)

        def e1_values(m):
            adder = nc.vector if m <= CHUNKS_AHEAD else nc.gpsimd
            b, i0 = divmod(m * CHUNK_I, N)
            shape = [P, CHUNK_I, N, PACK]
            if m < CHUNKS_AHEAD:
                pre = work.tile(shape, F32, tag="pre_start", bufs=2)
            else:
                pre = work.tile(shape, F32, tag="pre_round", bufs=1)
            adder.tensor_tensor(
                out=pre[:],
                in0=u_b0[:, b * N + i0 : b * N + i0 + CHUNK_I, :].unsqueeze(2).to_broadcast(shape),
                in1=v_sb[:, b * N : (b + 1) * N, :].unsqueeze(1).to_broadcast(shape),
                op=ALU.add,
            )
            pre_flat = pre[:].rearrange("p i j t -> p (i j t)")
            e1 = work.tile([P, CHUNK * PACK], BF16, tag="e1", align_bytes=64)
            nc.vector.scalar_tensor_tensor(
                out=e1[:], in0=pre_flat, scalar=ALPHA, in1=pre_flat, op0=ALU.mult, op1=ALU.max
            )
            return e1

        def e1_quantise(m, e1):
            cols = slice(m * CHUNK, (m + 1) * CHUNK)
            nc.vector.quantize_mx(out=e1_codes[:, cols].bitcast(FP8X4), scales=e1_scales[:, cols], in_=e1[:])

        def multiply(n):
            pairs, half = divmod(n, HALVES)
            codes, scales = w1_q[half]
            cols = slice(pairs * ROUND_PAIRS, (pairs + 1) * ROUND_PAIRS)
            banks = []
            for k in range(ROUND_BLOCKS):
                acc = sums.tile([P, ROUND_PAIRS], F32, tag="sums")
                nc.tensor.matmul_mx(
                    out=acc[:],
                    lhsT=codes[:, k * P : (k + 1) * P].bitcast(FP8X4),
                    lhsT_scale=scales[:, k * P : (k + 1) * P],
                    rhs=e1_codes[:, cols].bitcast(FP8X4),
                    rhs_scale=e1_scales[:, cols],
                    start=True,
                    stop=True,
                )
                banks.append(acc)
            return banks

        def add_bias(n, banks):
            half = n % HALVES
            if n + CHUNKS_AHEAD > CHUNKS:
                vector_cols = 2 * ROUND_PAIRS
            elif n > 0:
                vector_cols = 3 * ROUND_PAIRS // 4
            else:
                vector_cols = 0
            tiles = []
            for k in range(ROUND_BLOCKS):
                column = B0_ROWS + half * ROUND_BLOCKS + k
                z = biased.tile([P, ROUND_PAIRS], F32, tag="z")
                split = min(max((ROUND_BLOCKS - k) * ROUND_PAIRS - vector_cols, 0), ROUND_PAIRS)
                if split > 0:
                    nc.scalar.activation(
                        out=z[:, 0:split],
                        in_=banks[k][:, 0:split],
                        func=ACT.Identity,
                        bias=bias[:, column : column + 1],
                        scale=1.0,
                    )
                if split < ROUND_PAIRS:
                    nc.vector.tensor_scalar_add(
                        out=z[:, split:ROUND_PAIRS], in0=banks[k][:, split:ROUND_PAIRS], scalar1=bias[:, column : column + 1]
                    )
                tiles.append(z)
            return tiles

        def turn(tiles):
            banks = []
            for s in range(ROUND_BLOCKS):
                z_turned = turned.tile([P, BANK], F32, tag="turned")
                for k in range(ROUND_BLOCKS):
                    nc.tensor.transpose(
                        z_turned[:, k * P : (k + 1) * P], tiles[k][:, s * P : (s + 1) * P], ident_f32[:]
                    )
                banks.append(z_turned)
            return banks

        def lrelu_and_store(n, s, z_turned):
            pairs, half = divmod(n, HALVES)
            scaled = result.tile([P, BANK], F32, tag="scaled")
            nc.scalar.mul(out=scaled[:], in_=z_turned[:], mul=ALPHA)
            res = result.tile([P, BANK], F32, tag="res")
            nc.vector.tensor_tensor(out=res[:], in0=z_turned[:], in1=scaled[:], op=ALU.max)
            row0 = pairs * ROUND_PAIRS + s * P
            nc.sync.dma_start(out=out_rows[row0 : row0 + P, half * BANK : (half + 1) * BANK], in_=res[:])

        early = [e1_values(0)]
        w1_q = [quantise(w1_grouped[0], BANK, "w1a")]
        early.append(e1_values(1))
        e1_quantise(0, early[0])
        e1_quantise(1, early[1])
        banks = multiply(0)
        z_tiles = add_bias(0, banks)
        w1_q.append(quantise(w1_grouped[1], BANK, "w1b"))
        early.append(e1_values(2))
        early.append(e1_values(3))
        e1_quantise(2, early[2])
        e1_quantise(3, early[3])

        for n in range(ROUNDS):
            m = n + CHUNKS_AHEAD
            if m < CHUNKS:
                e1 = e1_values(m)
            if n + 1 < ROUNDS:
                banks = multiply(n + 1)
            turned_banks = turn(z_tiles)
            if n + 1 < ROUNDS:
                z_tiles = add_bias(n + 1, banks)
            for s in range(ROUND_BLOCKS):
                lrelu_and_store(n, s, turned_banks[s])
            if m < CHUNKS:
                e1_quantise(m, e1)
